import numpy as np
import ml_dtypes


def mxq(x, axis, fmt="e4m3"):
    dtype, down = {"e4m3": (ml_dtypes.float8_e4m3fn, 7), "e5m2": (ml_dtypes.float8_e5m2, 14)}[fmt]
    v = np.moveaxis(np.asarray(x, np.float32).astype(ml_dtypes.bfloat16).astype(np.float64), axis, -1)
    blocks = v.reshape(v.shape[:-1] + (-1, 32))
    amax = np.abs(blocks).max(-1, keepdims=True)
    byte = np.maximum(np.where(amax > 0, np.frexp(amax)[1] - 1 + 127, 0) - down, 1)
    scale = np.exp2(byte - 127.0)
    codes = (blocks / scale).astype(np.float32).astype(dtype).astype(np.float64)
    return np.moveaxis((codes * scale).reshape(v.shape), -1, axis)


WIDE = False


def mx_kscale(k):
    if not WIDE:
        return np.ones(k)
    levels = np.array([10, -10, 5, -5, 0])
    if k % 512:
        return np.exp2(np.random.permutation(np.resize(levels, k // 32))).repeat(32)
    a = np.empty((k // 512, 16))
    for p in range(k // 512):
        a[p, :8] = np.random.permutation(np.resize(levels, 8))
        for g in range(8):
            far = levels[np.abs(levels - a[p, g]) >= 10]
            a[p, g + 8] = far[np.random.randint(len(far))]
    return np.exp2(a.ravel()).repeat(32)


BF16 = ml_dtypes.bfloat16


def bf(x):
    return np.asarray(x, np.float32).astype(BF16)


def f64(x):
    return np.asarray(x).astype(np.float64)


B, S, IN, OUT, A, R = 8, 128, 1024, 128, 8, 128
G = B // A
SCALING = 2.0


def setup_inputs():
    s = mx_kscale(IN)
    return {"data": bf(np.random.standard_normal((B, S, IN)) * s),
            "W": bf(np.random.standard_normal((OUT, IN)) / np.sqrt(IN) / s),
            "t_lora": bf(np.random.standard_normal((A, G, S, R))),
            "lora_b": bf(np.random.standard_normal((A, OUT, R)) * 0.5 / np.sqrt(R))}


def reference(data, W, t_lora, lora_b):
    base = mxq(f64(data), 2, "e4m3") @ mxq(f64(W), 1, "e4m3").T
    delta = (f64(t_lora).reshape(A, G * S, R) @ f64(lora_b).transpose(0, 2, 1)) * SCALING
    return base + delta.reshape(B, S, OUT)

@@ -1,0 +1,167 @@
+from contextlib import ExitStack
+
+import concourse.mybir as mybir
+from concourse.masks import make_identity
+
+BF16 = mybir.dt.bfloat16
+F32 = mybir.dt.float32
+U32 = mybir.dt.uint32
+U8 = mybir.dt.uint8
+FP8X4 = mybir.dt.float8_e4m3fn_x4
+
+P = 128
+B, S, IN, OUT, R = 8, 128, 1024, 128, 128
+SCALING = 2.0
+
+PACK = 4
+K_PASS = P * PACK
+PASSES = IN // K_PASS
+PAIR = 2
+WORD_BLOCKS = IN // (PAIR * P)
+BLOCKS_PER_PASS = WORD_BLOCKS // PASSES
+ADAPTERS_PER_BANK = 4
+ROUND = 2
+ROUNDS = B // ROUND
+LEAD = 2
+WARM_PASSES = 8
+
+FLOPS = 2 * B * S * IN * OUT + 2 * B * S * R * OUT
+
+
+def quantise_rows(nc, psum, stage, ident_f32, rows, codes, scales):
+    words = rows.bitcast(F32)
+    flipped = psum.tile([P, WORD_BLOCKS, P], F32, tag="bank")
+    span = BLOCKS_PER_PASS * P
+    for j in range(WORD_BLOCKS):
+        g, u = divmod(j, BLOCKS_PER_PASS)
+        nc.tensor.transpose(
+            flipped[:, j, :], words[:, g * span + u : (g + 1) * span : BLOCKS_PER_PASS], ident_f32[:]
+        )
+    grouped = stage.tile([P, PASSES * P * PACK], BF16, align_bytes=64)
+    nc.scalar.copy(
+        out=grouped[:].bitcast(F32).rearrange("p (g r u) -> p g r u", g=PASSES, u=BLOCKS_PER_PASS),
+        in_=flipped[:].rearrange("p (g u) r -> p g r u", u=BLOCKS_PER_PASS),
+    )
+    nc.vector.quantize_mx(out=codes.bitcast(FP8X4), scales=scales, in_=grouped[:])
+
+
+def tile_linear_pa_s_kernel(tc, data, W, t_lora, lora_b, out):
+    nc = tc.nc
+    with ExitStack() as ctx:
+        keep = ctx.enter_context(tc.tile_pool(name="keep", bufs=1))
+        stage = ctx.enter_context(tc.tile_pool(name="stage", bufs=(LEAD + 1) * ROUND))
+        psum = ctx.enter_context(tc.psum_pool(name="psum", bufs=8))
+
+        ident_f32 = keep.tile([P, P], F32)
+        make_identity(nc, ident_f32[:])
+        ident_bf16 = keep.tile([P, P], BF16)
+        make_identity(nc, ident_bf16[:])
+
+        w_sb = keep.tile([P, IN], BF16)
+        nc.sync.dma_start(out=w_sb[:], in_=W[:, :])
+        x_sb = keep.tile([P, B, IN], BF16)
+        for b in range(B):
+            nc.sync.dma_start(out=x_sb[:, b, :], in_=data[b, :, :])
+        t_sb = keep.tile([P, B, R], BF16)
+        b_sb = keep.tile([P, B, R], BF16)
+        for first in range(0, B, ADAPTERS_PER_BANK):
+            these = slice(first, first + ADAPTERS_PER_BANK)
+            nc.sync.dma_start(
+                out=t_sb[:, these, :], in_=t_lora[these].rearrange("a g s r -> s (a g) r")
+            )
+            nc.sync.dma_start(out=b_sb[:, these, :], in_=lora_b[these].rearrange("a o r -> o a r"))
+
+        w_codes = keep.tile([P, PASSES * OUT], U32, align_bytes=64)
+        w_scales = keep.tile([P, PASSES * OUT], U8, align_bytes=64)
+        x_codes = keep.tile([P, B, PASSES * S], U32, align_bytes=64)
+        x_scales = keep.tile([P, B, PASSES * S], U8, align_bytes=64)
+        base = keep.tile([P, B, OUT], F32)
+        tbT = keep.tile([P, B, 2, P], BF16)
+        result = keep.tile([P, B, OUT], F32)
+
+        def quantise_round(first):
+            for b in range(first, first + ROUND):
+                quantise_rows(
+                    nc, psum, stage, ident_f32, x_sb[:, b, :], x_codes[:, b, :], x_scales[:, b, :]
+                )
+
+        def multiply_round(first):
+            acc = psum.tile([P, ROUND, OUT], F32, tag="bank")
+            for i in range(ROUND):
+                b = first + i
+                for g in range(PASSES):
+                    nc.tensor.matmul_mx(
+                        out=acc[:, i, :],
+                        lhsT=x_codes[:, b, g * S : (g + 1) * S].bitcast(FP8X4),
+                        lhsT_scale=x_scales[:, b, g * S : (g + 1) * S],
+                        rhs=w_codes[:, g * OUT : (g + 1) * OUT].bitcast(FP8X4),
+                        rhs_scale=w_scales[:, g * OUT : (g + 1) * OUT],
+                        start=(g == 0),
+                        stop=(g == PASSES - 1),
+                    )
+            nc.vector.tensor_copy(out=base[:, first : first + ROUND, :], in_=acc[:])
+
+        def flip_adapters(first):
+            tbT_ps = psum.tile([P, ROUND, 2, P], BF16, tag="bank")
+            for i in range(ROUND):
+                nc.tensor.transpose(tbT_ps[:, i, 0, :], t_sb[:, first + i, :], ident_bf16[:])
+                nc.tensor.transpose(tbT_ps[:, i, 1, :], b_sb[:, first + i, :], ident_bf16[:])
+            nc.scalar.copy(out=tbT[:, first : first + ROUND, :, :], in_=tbT_ps[:])
+
+        def add_adapters(first):
+            these = slice(first, first + ROUND)
+            delta_ps = psum.tile([P, ROUND, OUT], F32, tag="bank")
+            for i in range(ROUND):
+                nc.tensor.matmul(
+                    delta_ps[:, i, :],
+                    lhsT=tbT[:, first + i, 0, :],
+                    rhs=tbT[:, first + i, 1, :],
+                    start=True,
+                    stop=True,
+                )
+            nc.vector.scalar_tensor_tensor(
+                out=result[:, these, :],
+                in0=delta_ps[:],
+                scalar=SCALING,
+                in1=base[:, these, :],
+                op0=mybir.AluOpType.mult,
+                op1=mybir.AluOpType.add,
+            )
+            nc.sync.dma_start(out=out[these].rearrange("b s o -> s b o"), in_=result[:, these, :])
+
+        with tc.manual_schedule():
+            zeros = keep.tile([P, P * PACK], BF16, align_bytes=64)
+            nc.vector.memset(zeros[:], 0.0)
+            zero_codes = keep.tile([P, P], U32, align_bytes=64)
+            zero_scales = keep.tile([P, P], U8, align_bytes=64)
+            nc.vector.quantize_mx(
+                out=zero_codes[:].bitcast(FP8X4), scales=zero_scales[:], in_=zeros[:]
+            )
+
+            def spin():
+                warm_ps = psum.tile([P, P], F32, tag="bank")
+                for i in range(WARM_PASSES):
+                    nc.tensor.matmul_mx(
+                        out=warm_ps[:],
+                        lhsT=zero_codes[:].bitcast(FP8X4),
+                        lhsT_scale=zero_scales[:],
+                        rhs=zero_codes[:].bitcast(FP8X4),
+                        rhs_scale=zero_scales[:],
+                        start=True,
+                        stop=True,
+                    )
+
+            spin()
+            quantise_rows(nc, psum, stage, ident_f32, w_sb[:], w_codes[:], w_scales[:])
+            for step in range(2 * ROUNDS + LEAD):
+                if step < ROUNDS:
+                    quantise_round(step * ROUND)
+                elif step < 2 * ROUNDS:
+                    flip_adapters((step - ROUNDS) * ROUND)
+                due = step - LEAD
+                if due < 0:
+                    spin()
+                elif due < ROUNDS:
+                    multiply_round(due * ROUND)
+                elif due >= ROUNDS:
+                    add_adapters((due - ROUNDS) * ROUND)

@@ -22,34 +22,40 @@ BLOCKS_PER_PASS = WORD_BLOCKS // PASSES
 ADAPTERS_PER_BANK = 4
 ROUND = 2
 ROUNDS = B // ROUND
-LEAD = 2
-WARM_PASSES = 8
+LEAD = 1
+WARM_PASSES = 12
+SORTED = ()
 
 FLOPS = 2 * B * S * IN * OUT + 2 * B * S * R * OUT
 
 
-def quantise_rows(nc, psum, stage, ident_f32, rows, codes, scales):
-    words = rows.bitcast(F32)
+def flip_rows(nc, psum, ident_f32, words, sorted_words):
     flipped = psum.tile([P, WORD_BLOCKS, P], F32, tag="bank")
     span = BLOCKS_PER_PASS * P
     for j in range(WORD_BLOCKS):
         g, u = divmod(j, BLOCKS_PER_PASS)
-        nc.tensor.transpose(
-            flipped[:, j, :], words[:, g * span + u : (g + 1) * span : BLOCKS_PER_PASS], ident_f32[:]
-        )
+        if sorted_words:
+            block = words[:, j * P : (j + 1) * P]
+        else:
+            block = words[:, g * span + u : (g + 1) * span : BLOCKS_PER_PASS]
+        nc.tensor.transpose(flipped[:, j, :], block, ident_f32[:])
+    return flipped
+
+
+def lay_side_by_side(stage, copy, flipped):
     grouped = stage.tile([P, PASSES * P * PACK], BF16, align_bytes=64)
-    nc.scalar.copy(
+    copy(
         out=grouped[:].bitcast(F32).rearrange("p (g r u) -> p g r u", g=PASSES, u=BLOCKS_PER_PASS),
         in_=flipped[:].rearrange("p (g u) r -> p g r u", u=BLOCKS_PER_PASS),
     )
-    nc.vector.quantize_mx(out=codes.bitcast(FP8X4), scales=scales, in_=grouped[:])
+    return grouped
 
 
 def tile_linear_pa_s_kernel(tc, data, W, t_lora, lora_b, out):
     nc = tc.nc
     with ExitStack() as ctx:
         keep = ctx.enter_context(tc.tile_pool(name="keep", bufs=1))
-        stage = ctx.enter_context(tc.tile_pool(name="stage", bufs=(LEAD + 1) * ROUND))
+        stage = ctx.enter_context(tc.tile_pool(name="stage", bufs=4))
         psum = ctx.enter_context(tc.psum_pool(name="psum", bufs=8))
 
         ident_f32 = keep.tile([P, P], F32)
@@ -79,11 +85,26 @@ def tile_linear_pa_s_kernel(tc, data, W, t_lora, lora_b, out):
         tbT = keep.tile([P, B, 2, P], BF16)
         result = keep.tile([P, B, OUT], F32)
 
+        def sort_words(b):
+            tile = stage.tile([P, IN // PAIR], F32, tag="sorted")
+            nc.vector.tensor_copy(
+                out=tile[:].rearrange("p (g u w) -> p g u w", g=PASSES, u=BLOCKS_PER_PASS),
+                in_=x_sb[:, b, :]
+                .bitcast(F32)
+                .rearrange("p (g w u) -> p g u w", g=PASSES, u=BLOCKS_PER_PASS),
+            )
+            return tile
+
+        def quantise(flipped, codes, scales):
+            grouped = lay_side_by_side(stage, nc.scalar.copy, flipped)
+            nc.vector.quantize_mx(out=codes.bitcast(FP8X4), scales=scales, in_=grouped[:])
+
         def quantise_round(first):
-            for b in range(first, first + ROUND):
-                quantise_rows(
-                    nc, psum, stage, ident_f32, x_sb[:, b, :], x_codes[:, b, :], x_scales[:, b, :]
-                )
+            rows = range(first, first + ROUND)
+            words = [sort_words(b)[:] if b in SORTED else x_sb[:, b, :].bitcast(F32) for b in rows]
+            flipped = [flip_rows(nc, psum, ident_f32, w, b in SORTED) for b, w in zip(rows, words)]
+            for b, tile in zip(rows, flipped):
+                quantise(tile, x_codes[:, b, :], x_scales[:, b, :])
 
         def multiply_round(first):
             acc = psum.tile([P, ROUND, OUT], F32, tag="bank")
@@ -99,14 +120,14 @@ def tile_linear_pa_s_kernel(tc, data, W, t_lora, lora_b, out):
                         start=(g == 0),
                         stop=(g == PASSES - 1),
                     )
-            nc.vector.tensor_copy(out=base[:, first : first + ROUND, :], in_=acc[:])
+            nc.scalar.copy(out=base[:, first : first + ROUND, :], in_=acc[:])
 
         def flip_adapters(first):
             tbT_ps = psum.tile([P, ROUND, 2, P], BF16, tag="bank")
             for i in range(ROUND):
                 nc.tensor.transpose(tbT_ps[:, i, 0, :], t_sb[:, first + i, :], ident_bf16[:])
                 nc.tensor.transpose(tbT_ps[:, i, 1, :], b_sb[:, first + i, :], ident_bf16[:])
-            nc.scalar.copy(out=tbT[:, first : first + ROUND, :, :], in_=tbT_ps[:])
+            nc.vector.tensor_copy(out=tbT[:, first : first + ROUND, :, :], in_=tbT_ps[:])
 
         def add_adapters(first):
             these = slice(first, first + ROUND)
@@ -152,16 +173,16 @@ def tile_linear_pa_s_kernel(tc, data, W, t_lora, lora_b, out):
                     )
 
             spin()
-            quantise_rows(nc, psum, stage, ident_f32, w_sb[:], w_codes[:], w_scales[:])
-            for step in range(2 * ROUNDS + LEAD):
+            quantise(flip_rows(nc, psum, ident_f32, w_sb[:].bitcast(F32), False), w_codes[:], w_scales[:])
+            for step in range(ROUNDS + LEAD):
                 if step < ROUNDS:
                     quantise_round(step * ROUND)
-                elif step < 2 * ROUNDS:
-                    flip_adapters((step - ROUNDS) * ROUND)
-                due = step - LEAD
-                if due < 0:
-                    spin()
-                elif due < ROUNDS:
-                    multiply_round(due * ROUND)
-                elif due >= ROUNDS:
-                    add_adapters((due - ROUNDS) * ROUND)
+                else:
+                    flip_adapters(0)
+                    flip_adapters(ROUND)
+                if step >= LEAD:
+                    multiply_round((step - LEAD) * ROUND)
+            flip_adapters(2 * ROUND)
+            flip_adapters(3 * ROUND)
+            for r in range(ROUNDS):
+                add_adapters(r * ROUND)

@@ -14,41 +14,17 @@ B, S, IN, OUT, R = 8, 128, 1024, 128, 128
 SCALING = 2.0
 
 PACK = 4
-K_PASS = P * PACK
-PASSES = IN // K_PASS
+PASSES = IN // (P * PACK)
 PAIR = 2
-WORD_BLOCKS = IN // (PAIR * P)
-BLOCKS_PER_PASS = WORD_BLOCKS // PASSES
-ADAPTERS_PER_BANK = 4
-ROUND = 2
-ROUNDS = B // ROUND
-LEAD = 1
-WARM_PASSES = 12
-SORTED = ()
+WORDS = IN // PAIR
+HALVES = PACK // PAIR
+BANK = 4
+STORE = 2
+WARM_PASSES = 14
+HOLD_PASSES = 4
+WORK_BANKS = 5
 
 FLOPS = 2 * B * S * IN * OUT + 2 * B * S * R * OUT
-
-
-def flip_rows(nc, psum, ident_f32, words, sorted_words):
-    flipped = psum.tile([P, WORD_BLOCKS, P], F32, tag="bank")
-    span = BLOCKS_PER_PASS * P
-    for j in range(WORD_BLOCKS):
-        g, u = divmod(j, BLOCKS_PER_PASS)
-        if sorted_words:
-            block = words[:, j * P : (j + 1) * P]
-        else:
-            block = words[:, g * span + u : (g + 1) * span : BLOCKS_PER_PASS]
-        nc.tensor.transpose(flipped[:, j, :], block, ident_f32[:])
-    return flipped
-
-
-def lay_side_by_side(stage, copy, flipped):
-    grouped = stage.tile([P, PASSES * P * PACK], BF16, align_bytes=64)
-    copy(
-        out=grouped[:].bitcast(F32).rearrange("p (g r u) -> p g r u", g=PASSES, u=BLOCKS_PER_PASS),
-        in_=flipped[:].rearrange("p (g u) r -> p g r u", u=BLOCKS_PER_PASS),
-    )
-    return grouped
 
 
 def tile_linear_pa_s_kernel(tc, data, W, t_lora, lora_b, out):
@@ -56,7 +32,7 @@ def tile_linear_pa_s_kernel(tc, data, W, t_lora, lora_b, out):
     with ExitStack() as ctx:
         keep = ctx.enter_context(tc.tile_pool(name="keep", bufs=1))
         stage = ctx.enter_context(tc.tile_pool(name="stage", bufs=4))
-        psum = ctx.enter_context(tc.psum_pool(name="psum", bufs=8))
+        psum = ctx.enter_context(tc.psum_pool(name="psum", bufs=1))
 
         ident_f32 = keep.tile([P, P], F32)
         make_identity(nc, ident_f32[:])
@@ -64,106 +40,129 @@ def tile_linear_pa_s_kernel(tc, data, W, t_lora, lora_b, out):
         make_identity(nc, ident_bf16[:])
 
         w_sb = keep.tile([P, IN], BF16)
-        nc.sync.dma_start(out=w_sb[:], in_=W[:, :])
         x_sb = keep.tile([P, B, IN], BF16)
-        for b in range(B):
-            nc.sync.dma_start(out=x_sb[:, b, :], in_=data[b, :, :])
         t_sb = keep.tile([P, B, R], BF16)
         b_sb = keep.tile([P, B, R], BF16)
-        for first in range(0, B, ADAPTERS_PER_BANK):
-            these = slice(first, first + ADAPTERS_PER_BANK)
+
+        def load_adapters(first, count):
+            these = slice(first, first + count)
             nc.sync.dma_start(
                 out=t_sb[:, these, :], in_=t_lora[these].rearrange("a g s r -> s (a g) r")
             )
             nc.sync.dma_start(out=b_sb[:, these, :], in_=lora_b[these].rearrange("a o r -> o a r"))
 
+        nc.sync.dma_start(out=w_sb[:], in_=W[:, :])
+        for b in range(B):
+            nc.sync.dma_start(out=x_sb[:, b, :], in_=data[b, :, :])
+        for first in range(0, B, BANK):
+            load_adapters(first, BANK)
+
         w_codes = keep.tile([P, PASSES * OUT], U32, align_bytes=64)
         w_scales = keep.tile([P, PASSES * OUT], U8, align_bytes=64)
         x_codes = keep.tile([P, B, PASSES * S], U32, align_bytes=64)
         x_scales = keep.tile([P, B, PASSES * S], U8, align_bytes=64)
-        base = keep.tile([P, B, OUT], F32)
         tbT = keep.tile([P, B, 2, P], BF16)
+        base = keep.tile([P, B, OUT], F32)
         result = keep.tile([P, B, OUT], F32)
 
         def sort_words(b):
-            tile = stage.tile([P, IN // PAIR], F32, tag="sorted")
+            tile = stage.tile([P, WORDS], F32, tag="sorted", name="sorted_words")
             nc.vector.tensor_copy(
-                out=tile[:].rearrange("p (g u w) -> p g u w", g=PASSES, u=BLOCKS_PER_PASS),
-                in_=x_sb[:, b, :]
-                .bitcast(F32)
-                .rearrange("p (g w u) -> p g u w", g=PASSES, u=BLOCKS_PER_PASS),
+                out=tile[:].rearrange("p (g u w) -> p g u w", g=PASSES, u=HALVES),
+                in_=x_sb[:, b, :].bitcast(F32).rearrange("p (g w u) -> p g u w", g=PASSES, u=HALVES),
             )
-            return tile
+            return tile[:]
 
-        def quantise(flipped, codes, scales):
-            grouped = lay_side_by_side(stage, nc.scalar.copy, flipped)
+        def flip(words, in_order):
+            bank = psum.tile([P, PASSES * HALVES, P], F32, tag="work", bufs=WORK_BANKS)
+            for g in range(PASSES):
+                for u in range(HALVES):
+                    start = g * HALVES * P
+                    if in_order:
+                        block = words[:, start + u * P : start + (u + 1) * P]
+                    else:
+                        block = words[:, start + u : start + HALVES * P : HALVES]
+                    nc.tensor.transpose(bank[:, g * HALVES + u, :], block, ident_f32[:])
+            return bank
+
+        def regroup(copy, bank):
+            grouped = stage.tile([P, PASSES * P * PACK], BF16, align_bytes=64)
+            copy(
+                out=grouped[:].bitcast(F32).rearrange("p (g r u) -> p g r u", g=PASSES, u=HALVES),
+                in_=bank[:].rearrange("p (g u) r -> p g r u", u=HALVES),
+            )
+            return grouped
+
+        def quantise(grouped, codes, scales):
             nc.vector.quantize_mx(out=codes.bitcast(FP8X4), scales=scales, in_=grouped[:])
 
-        def quantise_round(first):
-            rows = range(first, first + ROUND)
-            words = [sort_words(b)[:] if b in SORTED else x_sb[:, b, :].bitcast(F32) for b in rows]
-            flipped = [flip_rows(nc, psum, ident_f32, w, b in SORTED) for b, w in zip(rows, words)]
-            for b, tile in zip(rows, flipped):
-                quantise(tile, x_codes[:, b, :], x_scales[:, b, :])
+        def flip_row(b, words=None):
+            if words is None:
+                bank = flip(x_sb[:, b, :].bitcast(F32), False)
+            else:
+                bank = flip(words, True)
+            return regroup(nc.scalar.copy, bank)
 
-        def multiply_round(first):
-            acc = psum.tile([P, ROUND, OUT], F32, tag="bank")
-            for i in range(ROUND):
-                b = first + i
-                for g in range(PASSES):
-                    nc.tensor.matmul_mx(
-                        out=acc[:, i, :],
-                        lhsT=x_codes[:, b, g * S : (g + 1) * S].bitcast(FP8X4),
-                        lhsT_scale=x_scales[:, b, g * S : (g + 1) * S],
-                        rhs=w_codes[:, g * OUT : (g + 1) * OUT].bitcast(FP8X4),
-                        rhs_scale=w_scales[:, g * OUT : (g + 1) * OUT],
-                        start=(g == 0),
-                        stop=(g == PASSES - 1),
-                    )
-            nc.scalar.copy(out=base[:, first : first + ROUND, :], in_=acc[:])
+        def quantise_row(b, grouped):
+            quantise(grouped, x_codes[:, b, :], x_scales[:, b, :])
+
+        def multiply(acc, b):
+            for g in range(PASSES):
+                nc.tensor.matmul_mx(
+                    out=acc[:, b % BANK, :],
+                    lhsT=x_codes[:, b, g * S : (g + 1) * S].bitcast(FP8X4),
+                    lhsT_scale=x_scales[:, b, g * S : (g + 1) * S],
+                    rhs=w_codes[:, g * OUT : (g + 1) * OUT].bitcast(FP8X4),
+                    rhs_scale=w_scales[:, g * OUT : (g + 1) * OUT],
+                    start=(g == 0),
+                    stop=(g == PASSES - 1),
+                )
 
         def flip_adapters(first):
-            tbT_ps = psum.tile([P, ROUND, 2, P], BF16, tag="bank")
-            for i in range(ROUND):
-                nc.tensor.transpose(tbT_ps[:, i, 0, :], t_sb[:, first + i, :], ident_bf16[:])
-                nc.tensor.transpose(tbT_ps[:, i, 1, :], b_sb[:, first + i, :], ident_bf16[:])
-            nc.vector.tensor_copy(out=tbT[:, first : first + ROUND, :, :], in_=tbT_ps[:])
+            bank = psum.tile([P, 2, 2, P], BF16, tag="work", bufs=WORK_BANKS)
+            for i in range(2):
+                nc.tensor.transpose(bank[:, i, 0, :], t_sb[:, first + i, :], ident_bf16[:])
+                nc.tensor.transpose(bank[:, i, 1, :], b_sb[:, first + i, :], ident_bf16[:])
+            nc.vector.tensor_copy(out=tbT[:, first : first + 2, :, :], in_=bank[:])
 
-        def add_adapters(first):
-            these = slice(first, first + ROUND)
-            delta_ps = psum.tile([P, ROUND, OUT], F32, tag="bank")
-            for i in range(ROUND):
+        def finish(first):
+            bank = psum.tile([P, BANK, OUT], F32, tag="work", bufs=WORK_BANKS)
+            for i in range(BANK):
                 nc.tensor.matmul(
-                    delta_ps[:, i, :],
+                    bank[:, i, :],
                     lhsT=tbT[:, first + i, 0, :],
                     rhs=tbT[:, first + i, 1, :],
                     start=True,
                     stop=True,
                 )
-            nc.vector.scalar_tensor_tensor(
-                out=result[:, these, :],
-                in0=delta_ps[:],
-                scalar=SCALING,
-                in1=base[:, these, :],
-                op0=mybir.AluOpType.mult,
-                op1=mybir.AluOpType.add,
-            )
-            nc.sync.dma_start(out=out[these].rearrange("b s o -> s b o"), in_=result[:, these, :])
+            for i in range(0, BANK, STORE):
+                these = slice(first + i, first + i + STORE)
+                nc.vector.scalar_tensor_tensor(
+                    out=result[:, these, :],
+                    in0=bank[:, i : i + STORE, :],
+                    scalar=SCALING,
+                    in1=base[:, these, :],
+                    op0=mybir.AluOpType.mult,
+                    op1=mybir.AluOpType.add,
+                )
+                nc.sync.dma_start(
+                    out=out[these].rearrange("b s o -> s b o"), in_=result[:, these, :]
+                )
 
         with tc.manual_schedule():
             zeros = keep.tile([P, P * PACK], BF16, align_bytes=64)
-            nc.vector.memset(zeros[:], 0.0)
+            nc.vector.memset(zeros[:].bitcast(U32), 0)
             zero_codes = keep.tile([P, P], U32, align_bytes=64)
             zero_scales = keep.tile([P, P], U8, align_bytes=64)
             nc.vector.quantize_mx(
                 out=zero_codes[:].bitcast(FP8X4), scales=zero_scales[:], in_=zeros[:]
             )
 
-            def spin():
-                warm_ps = psum.tile([P, P], F32, tag="bank")
-                for i in range(WARM_PASSES):
+            def spin(count):
+                warm = psum.tile([P, P], F32, tag="warm", bufs=1)
+                for i in range(count):
                     nc.tensor.matmul_mx(
-                        out=warm_ps[:],
+                        out=warm[:],
                         lhsT=zero_codes[:].bitcast(FP8X4),
                         lhsT_scale=zero_scales[:],
                         rhs=zero_codes[:].bitcast(FP8X4),
@@ -172,17 +171,49 @@ def tile_linear_pa_s_kernel(tc, data, W, t_lora, lora_b, out):
                         stop=True,
                     )
 
-            spin()
-            quantise(flip_rows(nc, psum, ident_f32, w_sb[:].bitcast(F32), False), w_codes[:], w_scales[:])
-            for step in range(ROUNDS + LEAD):
-                if step < ROUNDS:
-                    quantise_round(step * ROUND)
-                else:
-                    flip_adapters(0)
-                    flip_adapters(ROUND)
-                if step >= LEAD:
-                    multiply_round((step - LEAD) * ROUND)
-            flip_adapters(2 * ROUND)
-            flip_adapters(3 * ROUND)
-            for r in range(ROUNDS):
-                add_adapters(r * ROUND)
+            acc = [psum.tile([P, BANK, OUT], F32, tag="mx", bufs=2, name="acc") for i in range(B // BANK)]
+
+            def flip_w():
+                bank = flip(w_sb[:].bitcast(F32), False)
+                return regroup(nc.scalar.copy, bank)
+
+            def multiply_rows(first, end):
+                for b in range(first, end):
+                    multiply(acc[b // BANK], b)
+
+            def keep_base(first):
+                nc.scalar.copy(out=base[:, first : first + BANK, :], in_=acc[first // BANK][:])
+
+            spin(WARM_PASSES)
+            w_grouped = flip_w()
+            grouped = {0: flip_row(0)}
+            words = {b: sort_words(b) for b in (1, 2)}
+            quantise(w_grouped, w_codes[:], w_scales[:])
+            spin(HOLD_PASSES)
+            for b in (1, 2):
+                grouped[b] = flip_row(b, words[b])
+            words[3] = sort_words(3)
+            quantise_row(0, grouped[0])
+            spin(HOLD_PASSES)
+            grouped[3] = flip_row(3, words[3])
+            quantise_row(1, grouped[1])
+            grouped[4] = flip_row(4)
+            quantise_row(2, grouped[2])
+            multiply_rows(0, 2)
+            for b in (5, 6):
+                grouped[b] = flip_row(b)
+                quantise_row(b - 2, grouped[b - 2])
+            multiply_rows(2, 4)
+            grouped[7] = flip_row(7)
+            for b in (5, 6, 7):
+                quantise_row(b, grouped[b])
+            keep_base(0)
+            flip_adapters(0)
+            flip_adapters(2)
+            multiply_rows(4, 7)
+            flip_adapters(4)
+            flip_adapters(6)
+            finish(0)
+            multiply_rows(7, 8)
+            keep_base(4)
+            finish(4)

@@ -20,7 +20,7 @@ WORDS = IN // PAIR
 HALVES = PACK // PAIR
 BANK = 4
 STORE = 2
-WARM_PASSES = 14
+WARM_PASSES = 12
 HOLD_PASSES = 4
 WORK_BANKS = 5
 
@@ -39,7 +39,7 @@ def tile_linear_pa_s_kernel(tc, data, W, t_lora, lora_b, out):
         ident_bf16 = keep.tile([P, P], BF16)
         make_identity(nc, ident_bf16[:])
 
-        w_sb = keep.tile([P, IN], BF16)
+        w_sb = [keep.tile([P, IN // PASSES], BF16, name=f"w_sb{g}") for g in range(PASSES)]
         x_sb = keep.tile([P, B, IN], BF16)
         t_sb = keep.tile([P, B, R], BF16)
         b_sb = keep.tile([P, B, R], BF16)
@@ -51,7 +51,8 @@ def tile_linear_pa_s_kernel(tc, data, W, t_lora, lora_b, out):
             )
             nc.sync.dma_start(out=b_sb[:, these, :], in_=lora_b[these].rearrange("a o r -> o a r"))
 
-        nc.sync.dma_start(out=w_sb[:], in_=W[:, :])
+        for g in range(PASSES):
+            nc.sync.dma_start(out=w_sb[g][:], in_=W[:, g * P * PACK : (g + 1) * P * PACK])
         for b in range(B):
             nc.sync.dma_start(out=x_sb[:, b, :], in_=data[b, :, :])
         for first in range(0, B, BANK):
@@ -73,15 +74,17 @@ def tile_linear_pa_s_kernel(tc, data, W, t_lora, lora_b, out):
             )
             return tile[:]
 
-        def flip(words, in_order):
+        def by_pass(words):
+            return [words[:, g * HALVES * P : (g + 1) * HALVES * P] for g in range(PASSES)]
+
+        def flip(passes, in_order):
             bank = psum.tile([P, PASSES * HALVES, P], F32, tag="work", bufs=WORK_BANKS)
             for g in range(PASSES):
                 for u in range(HALVES):
-                    start = g * HALVES * P
                     if in_order:
-                        block = words[:, start + u * P : start + (u + 1) * P]
+                        block = passes[g][:, u * P : (u + 1) * P]
                     else:
-                        block = words[:, start + u : start + HALVES * P : HALVES]
+                        block = passes[g][:, u::HALVES]
                     nc.tensor.transpose(bank[:, g * HALVES + u, :], block, ident_f32[:])
             return bank
 
@@ -98,9 +101,9 @@ def tile_linear_pa_s_kernel(tc, data, W, t_lora, lora_b, out):
 
         def flip_row(b, words=None):
             if words is None:
-                bank = flip(x_sb[:, b, :].bitcast(F32), False)
+                bank = flip(by_pass(x_sb[:, b, :].bitcast(F32)), False)
             else:
-                bank = flip(words, True)
+                bank = flip(by_pass(words), True)
             return regroup(nc.scalar.copy, bank)
 
         def quantise_row(b, grouped):
@@ -118,12 +121,12 @@ def tile_linear_pa_s_kernel(tc, data, W, t_lora, lora_b, out):
                     stop=(g == PASSES - 1),
                 )
 
-        def flip_adapters(first):
+        def flip_adapters(copy, first):
             bank = psum.tile([P, 2, 2, P], BF16, tag="work", bufs=WORK_BANKS)
             for i in range(2):
                 nc.tensor.transpose(bank[:, i, 0, :], t_sb[:, first + i, :], ident_bf16[:])
                 nc.tensor.transpose(bank[:, i, 1, :], b_sb[:, first + i, :], ident_bf16[:])
-            nc.vector.tensor_copy(out=tbT[:, first : first + 2, :, :], in_=bank[:])
+            copy(out=tbT[:, first : first + 2, :, :], in_=bank[:])
 
         def finish(first):
             bank = psum.tile([P, BANK, OUT], F32, tag="work", bufs=WORK_BANKS)
@@ -174,7 +177,7 @@ def tile_linear_pa_s_kernel(tc, data, W, t_lora, lora_b, out):
             acc = [psum.tile([P, BANK, OUT], F32, tag="mx", bufs=2, name="acc") for i in range(B // BANK)]
 
             def flip_w():
-                bank = flip(w_sb[:].bitcast(F32), False)
+                bank = flip([half[:].bitcast(F32) for half in w_sb], False)
                 return regroup(nc.scalar.copy, bank)
 
             def multiply_rows(first, end):
@@ -205,15 +208,15 @@ def tile_linear_pa_s_kernel(tc, data, W, t_lora, lora_b, out):
                 quantise_row(b - 2, grouped[b - 2])
             multiply_rows(2, 4)
             grouped[7] = flip_row(7)
-            for b in (5, 6, 7):
-                quantise_row(b, grouped[b])
             keep_base(0)
-            flip_adapters(0)
-            flip_adapters(2)
-            multiply_rows(4, 7)
-            flip_adapters(4)
-            flip_adapters(6)
-            finish(0)
-            multiply_rows(7, 8)
+            quantise_row(5, grouped[5])
+            quantise_row(6, grouped[6])
+            flip_adapters(nc.vector.tensor_copy, 0)
+            flip_adapters(nc.vector.tensor_copy, 2)
+            quantise_row(7, grouped[7])
+            flip_adapters(nc.vector.tensor_copy, 4)
+            flip_adapters(nc.vector.tensor_copy, 6)
+            multiply_rows(4, 8)
             keep_base(4)
+            finish(0)
             finish(4)

@@ -19,7 +19,6 @@ PAIR = 2
 WORDS = IN // PAIR
 HALVES = PACK // PAIR
 BANK = 4
-STORE = 2
 WARM_PASSES = 12
 HOLD_PASSES = 4
 WORK_BANKS = 5
@@ -74,36 +73,34 @@ def tile_linear_pa_s_kernel(tc, data, W, t_lora, lora_b, out):
             )
             return tile[:]
 
-        def by_pass(words):
-            return [words[:, g * HALVES * P : (g + 1) * HALVES * P] for g in range(PASSES)]
+        def flip_pass(half_bank, words, in_order):
+            for u in range(HALVES):
+                block = words[:, u * P : (u + 1) * P] if in_order else words[:, u::HALVES]
+                nc.tensor.transpose(half_bank[:, u, :], block, ident_f32[:])
 
-        def flip(passes, in_order):
+        def flip(words, in_order):
             bank = psum.tile([P, PASSES * HALVES, P], F32, tag="work", bufs=WORK_BANKS)
             for g in range(PASSES):
-                for u in range(HALVES):
-                    if in_order:
-                        block = passes[g][:, u * P : (u + 1) * P]
-                    else:
-                        block = passes[g][:, u::HALVES]
-                    nc.tensor.transpose(bank[:, g * HALVES + u, :], block, ident_f32[:])
+                words_of_pass = words[:, g * HALVES * P : (g + 1) * HALVES * P]
+                flip_pass(bank[:, g * HALVES : (g + 1) * HALVES, :], words_of_pass, in_order)
             return bank
 
         def regroup(copy, bank):
-            grouped = stage.tile([P, PASSES * P * PACK], BF16, align_bytes=64)
+            grouped = stage.tile([P, PASSES * P * PACK], BF16, align_bytes=64, tag="grouped")
             copy(
                 out=grouped[:].bitcast(F32).rearrange("p (g r u) -> p g r u", g=PASSES, u=HALVES),
                 in_=bank[:].rearrange("p (g u) r -> p g r u", u=HALVES),
             )
-            return grouped
+            return grouped[:]
 
         def quantise(grouped, codes, scales):
-            nc.vector.quantize_mx(out=codes.bitcast(FP8X4), scales=scales, in_=grouped[:])
+            nc.vector.quantize_mx(out=codes.bitcast(FP8X4), scales=scales, in_=grouped)
 
         def flip_row(b, words=None):
             if words is None:
-                bank = flip(by_pass(x_sb[:, b, :].bitcast(F32)), False)
+                bank = flip(x_sb[:, b, :].bitcast(F32), False)
             else:
-                bank = flip(by_pass(words), True)
+                bank = flip(words, True)
             return regroup(nc.scalar.copy, bank)
 
         def quantise_row(b, grouped):
@@ -128,7 +125,7 @@ def tile_linear_pa_s_kernel(tc, data, W, t_lora, lora_b, out):
                 nc.tensor.transpose(bank[:, i, 1, :], b_sb[:, first + i, :], ident_bf16[:])
             copy(out=tbT[:, first : first + 2, :, :], in_=bank[:])
 
-        def finish(first):
+        def adapt(first):
             bank = psum.tile([P, BANK, OUT], F32, tag="work", bufs=WORK_BANKS)
             for i in range(BANK):
                 nc.tensor.matmul(
@@ -138,19 +135,19 @@ def tile_linear_pa_s_kernel(tc, data, W, t_lora, lora_b, out):
                     start=True,
                     stop=True,
                 )
-            for i in range(0, BANK, STORE):
-                these = slice(first + i, first + i + STORE)
-                nc.vector.scalar_tensor_tensor(
-                    out=result[:, these, :],
-                    in0=bank[:, i : i + STORE, :],
-                    scalar=SCALING,
-                    in1=base[:, these, :],
-                    op0=mybir.AluOpType.mult,
-                    op1=mybir.AluOpType.add,
-                )
-                nc.sync.dma_start(
-                    out=out[these].rearrange("b s o -> s b o"), in_=result[:, these, :]
-                )
+            return bank
+
+        def finish(bank, first, count):
+            these = slice(first, first + count)
+            nc.vector.scalar_tensor_tensor(
+                out=result[:, these, :],
+                in0=bank[:, first % BANK : first % BANK + count, :],
+                scalar=SCALING,
+                in1=base[:, these, :],
+                op0=mybir.AluOpType.mult,
+                op1=mybir.AluOpType.add,
+            )
+            nc.sync.dma_start(out=out[these].rearrange("b s o -> s b o"), in_=result[:, these, :])
 
         with tc.manual_schedule():
             zeros = keep.tile([P, P * PACK], BF16, align_bytes=64)
@@ -177,46 +174,65 @@ def tile_linear_pa_s_kernel(tc, data, W, t_lora, lora_b, out):
             acc = [psum.tile([P, BANK, OUT], F32, tag="mx", bufs=2, name="acc") for i in range(B // BANK)]
 
             def flip_w():
-                bank = flip([half[:].bitcast(F32) for half in w_sb], False)
-                return regroup(nc.scalar.copy, bank)
+                grouped = stage.tile([P, PASSES, P * PACK], BF16, align_bytes=64, tag="grouped")
+                for g in range(PASSES):
+                    bank = psum.tile([P, HALVES, P], F32, tag="work", bufs=WORK_BANKS)
+                    flip_pass(bank, w_sb[g][:].bitcast(F32), False)
+                    nc.scalar.copy(
+                        out=grouped[:, g, :].bitcast(F32).rearrange("p (r u) -> p r u", u=HALVES),
+                        in_=bank[:].rearrange("p u r -> p r u"),
+                    )
+                return grouped[:].rearrange("p g c -> p (g c)")
 
             def multiply_rows(first, end):
                 for b in range(first, end):
                     multiply(acc[b // BANK], b)
 
-            def keep_base(first):
-                nc.scalar.copy(out=base[:, first : first + BANK, :], in_=acc[first // BANK][:])
+            def keep_base(first, count):
+                nc.scalar.copy(
+                    out=base[:, first : first + count, :],
+                    in_=acc[first // BANK][:, first % BANK : first % BANK + count, :],
+                )
 
             spin(WARM_PASSES)
             w_grouped = flip_w()
-            grouped = {0: flip_row(0)}
-            words = {b: sort_words(b) for b in (1, 2)}
+            words = {b: sort_words(b) for b in (0, 1, 2)}
+            grouped = {0: flip_row(0, words[0])}
             quantise(w_grouped, w_codes[:], w_scales[:])
+            grouped[1] = flip_row(1, words[1])
             spin(HOLD_PASSES)
-            for b in (1, 2):
-                grouped[b] = flip_row(b, words[b])
-            words[3] = sort_words(3)
+            grouped[2] = flip_row(2, words[2])
+            for b in (3, 4):
+                words[b] = sort_words(b)
             quantise_row(0, grouped[0])
+            words[5] = sort_words(5)
             spin(HOLD_PASSES)
             grouped[3] = flip_row(3, words[3])
             quantise_row(1, grouped[1])
-            grouped[4] = flip_row(4)
+            grouped[4] = flip_row(4, words[4])
             quantise_row(2, grouped[2])
             multiply_rows(0, 2)
-            for b in (5, 6):
-                grouped[b] = flip_row(b)
-                quantise_row(b - 2, grouped[b - 2])
+            grouped[5] = flip_row(5, words[5])
+            quantise_row(3, grouped[3])
+            grouped[6] = flip_row(6)
+            quantise_row(4, grouped[4])
             multiply_rows(2, 4)
             grouped[7] = flip_row(7)
-            keep_base(0)
+            keep_base(0, 4)
             quantise_row(5, grouped[5])
             quantise_row(6, grouped[6])
             flip_adapters(nc.vector.tensor_copy, 0)
             flip_adapters(nc.vector.tensor_copy, 2)
             quantise_row(7, grouped[7])
             flip_adapters(nc.vector.tensor_copy, 4)
-            flip_adapters(nc.vector.tensor_copy, 6)
+            flip_adapters(nc.scalar.copy, 6)
+            bank = adapt(0)
+            finish(bank, 0, 2)
+            finish(bank, 2, 2)
             multiply_rows(4, 8)
-            keep_base(4)
-            finish(0)
-            finish(4)
+            keep_base(4, 2)
+            keep_base(6, 2)
+            bank = adapt(4)
+            finish(bank, 4, 2)
+            finish(bank, 6, 1)
+            finish(bank, 7, 1)

@@ -21,7 +21,7 @@ HALVES = PACK // PAIR
 BANK = 4
 WARM_PASSES = 12
 HOLD_PASSES = 4
-WORK_BANKS = 5
+WORK_BANKS = 4
 
 FLOPS = 2 * B * S * IN * OUT + 2 * B * S * R * OUT
 
@@ -30,7 +30,7 @@ def tile_linear_pa_s_kernel(tc, data, W, t_lora, lora_b, out):
     nc = tc.nc
     with ExitStack() as ctx:
         keep = ctx.enter_context(tc.tile_pool(name="keep", bufs=1))
-        stage = ctx.enter_context(tc.tile_pool(name="stage", bufs=4))
+        stage = ctx.enter_context(tc.tile_pool(name="stage", bufs=6))
         psum = ctx.enter_context(tc.psum_pool(name="psum", bufs=1))
 
         ident_f32 = keep.tile([P, P], F32)
@@ -65,24 +65,15 @@ def tile_linear_pa_s_kernel(tc, data, W, t_lora, lora_b, out):
         base = keep.tile([P, B, OUT], F32)
         result = keep.tile([P, B, OUT], F32)
 
-        def sort_words(b):
-            tile = stage.tile([P, WORDS], F32, tag="sorted", name="sorted_words")
-            nc.vector.tensor_copy(
-                out=tile[:].rearrange("p (g u w) -> p g u w", g=PASSES, u=HALVES),
-                in_=x_sb[:, b, :].bitcast(F32).rearrange("p (g w u) -> p g u w", g=PASSES, u=HALVES),
-            )
-            return tile[:]
-
-        def flip_pass(half_bank, words, in_order):
+        def flip_pass(half_bank, words):
             for u in range(HALVES):
-                block = words[:, u * P : (u + 1) * P] if in_order else words[:, u::HALVES]
-                nc.tensor.transpose(half_bank[:, u, :], block, ident_f32[:])
+                nc.tensor.transpose(half_bank[:, u, :], words[:, u::HALVES], ident_f32[:])
 
-        def flip(words, in_order):
+        def flip(words):
             bank = psum.tile([P, PASSES * HALVES, P], F32, tag="work", bufs=WORK_BANKS)
             for g in range(PASSES):
                 words_of_pass = words[:, g * HALVES * P : (g + 1) * HALVES * P]
-                flip_pass(bank[:, g * HALVES : (g + 1) * HALVES, :], words_of_pass, in_order)
+                flip_pass(bank[:, g * HALVES : (g + 1) * HALVES, :], words_of_pass)
             return bank
 
         def regroup(copy, bank):
@@ -96,12 +87,8 @@ def tile_linear_pa_s_kernel(tc, data, W, t_lora, lora_b, out):
         def quantise(grouped, codes, scales):
             nc.vector.quantize_mx(out=codes.bitcast(FP8X4), scales=scales, in_=grouped)
 
-        def flip_row(b, words=None):
-            if words is None:
-                bank = flip(x_sb[:, b, :].bitcast(F32), False)
-            else:
-                bank = flip(words, True)
-            return regroup(nc.scalar.copy, bank)
+        def flip_row(b):
+            return regroup(nc.scalar.copy, flip(x_sb[:, b, :].bitcast(F32)))
 
         def quantise_row(b, grouped):
             quantise(grouped, x_codes[:, b, :], x_scales[:, b, :])
@@ -109,7 +96,7 @@ def tile_linear_pa_s_kernel(tc, data, W, t_lora, lora_b, out):
         def multiply(acc, b):
             for g in range(PASSES):
                 nc.tensor.matmul_mx(
-                    out=acc[:, b % BANK, :],
+                    out=acc[:, b % PAIR, :],
                     lhsT=x_codes[:, b, g * S : (g + 1) * S].bitcast(FP8X4),
                     lhsT_scale=x_scales[:, b, g * S : (g + 1) * S],
                     rhs=w_codes[:, g * OUT : (g + 1) * OUT].bitcast(FP8X4),
@@ -158,11 +145,15 @@ def tile_linear_pa_s_kernel(tc, data, W, t_lora, lora_b, out):
                 out=zero_codes[:].bitcast(FP8X4), scales=zero_scales[:], in_=zeros[:]
             )
 
+            acc = [
+                psum.tile([P, BANK, OUT], F32, tag="mx", bufs=B // PAIR, name="acc")
+                for i in range(B // PAIR)
+            ]
+
             def spin(count):
-                warm = psum.tile([P, P], F32, tag="warm", bufs=1)
                 for i in range(count):
                     nc.tensor.matmul_mx(
-                        out=warm[:],
+                        out=acc[-1][:, 0, :],
                         lhsT=zero_codes[:].bitcast(FP8X4),
                         lhsT_scale=zero_scales[:],
                         rhs=zero_codes[:].bitcast(FP8X4),
@@ -171,13 +162,12 @@ def tile_linear_pa_s_kernel(tc, data, W, t_lora, lora_b, out):
                         stop=True,
                     )
 
-            acc = [psum.tile([P, BANK, OUT], F32, tag="mx", bufs=2, name="acc") for i in range(B // BANK)]
 
             def flip_w():
                 grouped = stage.tile([P, PASSES, P * PACK], BF16, align_bytes=64, tag="grouped")
                 for g in range(PASSES):
                     bank = psum.tile([P, HALVES, P], F32, tag="work", bufs=WORK_BANKS)
-                    flip_pass(bank, w_sb[g][:].bitcast(F32), False)
+                    flip_pass(bank, w_sb[g][:].bitcast(F32))
                     nc.scalar.copy(
                         out=grouped[:, g, :].bitcast(F32).rearrange("p (r u) -> p r u", u=HALVES),
                         in_=bank[:].rearrange("p u r -> p r u"),
@@ -186,53 +176,50 @@ def tile_linear_pa_s_kernel(tc, data, W, t_lora, lora_b, out):
 
             def multiply_rows(first, end):
                 for b in range(first, end):
-                    multiply(acc[b // BANK], b)
+                    multiply(acc[b // PAIR], b)
 
-            def keep_base(first, count):
+            def keep_base(first):
                 nc.scalar.copy(
-                    out=base[:, first : first + count, :],
-                    in_=acc[first // BANK][:, first % BANK : first % BANK + count, :],
+                    out=base[:, first : first + PAIR, :], in_=acc[first // PAIR][:, :PAIR, :]
                 )
 
             spin(WARM_PASSES)
             w_grouped = flip_w()
-            words = {b: sort_words(b) for b in (0, 1, 2)}
-            grouped = {0: flip_row(0, words[0])}
+            grouped = {}
+            grouped[0] = flip_row(0)
+            spin(HOLD_PASSES)
             quantise(w_grouped, w_codes[:], w_scales[:])
-            grouped[1] = flip_row(1, words[1])
-            spin(HOLD_PASSES)
-            grouped[2] = flip_row(2, words[2])
-            for b in (3, 4):
-                words[b] = sort_words(b)
+            grouped[1] = flip_row(1)
             quantise_row(0, grouped[0])
-            words[5] = sort_words(5)
-            spin(HOLD_PASSES)
-            grouped[3] = flip_row(3, words[3])
+            grouped[2] = flip_row(2)
             quantise_row(1, grouped[1])
-            grouped[4] = flip_row(4, words[4])
+            grouped[3] = flip_row(3)
             quantise_row(2, grouped[2])
-            multiply_rows(0, 2)
-            grouped[5] = flip_row(5, words[5])
+            grouped[4] = flip_row(4)
             quantise_row(3, grouped[3])
-            grouped[6] = flip_row(6)
+            multiply_rows(0, 2)
+            spin(HOLD_PASSES)
+            keep_base(0)
+            grouped[5] = flip_row(5)
             quantise_row(4, grouped[4])
-            multiply_rows(2, 4)
-            grouped[7] = flip_row(7)
-            keep_base(0, 4)
+            grouped[6] = flip_row(6)
             quantise_row(5, grouped[5])
-            quantise_row(6, grouped[6])
+            grouped[7] = flip_row(7)
             flip_adapters(nc.vector.tensor_copy, 0)
             flip_adapters(nc.vector.tensor_copy, 2)
-            quantise_row(7, grouped[7])
-            flip_adapters(nc.vector.tensor_copy, 4)
+            multiply_rows(2, 4)
+            keep_base(2)
+            flip_adapters(nc.scalar.copy, 4)
+            quantise_row(6, grouped[6])
             flip_adapters(nc.scalar.copy, 6)
+            quantise_row(7, grouped[7])
             bank = adapt(0)
             finish(bank, 0, 2)
             finish(bank, 2, 2)
-            multiply_rows(4, 8)
-            keep_base(4, 2)
-            keep_base(6, 2)
+            multiply_rows(4, 6)
+            keep_base(4)
+            multiply_rows(6, 8)
+            keep_base(6)
             bank = adapt(4)
             finish(bank, 4, 2)
-            finish(bank, 6, 1)
-            finish(bank, 7, 1)
+            finish(bank, 6, 2)

@@ -19,9 +19,9 @@ PAIR = 2
 WORDS = IN // PAIR
 HALVES = PACK // PAIR
 BANK = 4
+GROUPS = [(0, 4), (4, 6), (6, 8)]
 WARM_PASSES = 12
-HOLD_PASSES = 4
-WORK_BANKS = 4
+WORK_BANKS = 5
 
 FLOPS = 2 * B * S * IN * OUT + 2 * B * S * R * OUT
 
@@ -93,10 +93,10 @@ def tile_linear_pa_s_kernel(tc, data, W, t_lora, lora_b, out):
         def quantise_row(b, grouped):
             quantise(grouped, x_codes[:, b, :], x_scales[:, b, :])
 
-        def multiply(acc, b):
+        def multiply(product, b):
             for g in range(PASSES):
                 nc.tensor.matmul_mx(
-                    out=acc[:, b % PAIR, :],
+                    out=product,
                     lhsT=x_codes[:, b, g * S : (g + 1) * S].bitcast(FP8X4),
                     lhsT_scale=x_scales[:, b, g * S : (g + 1) * S],
                     rhs=w_codes[:, g * OUT : (g + 1) * OUT].bitcast(FP8X4),
@@ -146,8 +146,8 @@ def tile_linear_pa_s_kernel(tc, data, W, t_lora, lora_b, out):
             )
 
             acc = [
-                psum.tile([P, BANK, OUT], F32, tag="mx", bufs=B // PAIR, name="acc")
-                for i in range(B // PAIR)
+                psum.tile([P, BANK, OUT], F32, tag="mx", bufs=len(GROUPS), name="acc")
+                for group in GROUPS
             ]
 
             def spin(count):
@@ -174,52 +174,58 @@ def tile_linear_pa_s_kernel(tc, data, W, t_lora, lora_b, out):
                     )
                 return grouped[:].rearrange("p g c -> p (g c)")
 
-            def multiply_rows(first, end):
+            def multiply_group(i):
+                first, end = GROUPS[i]
                 for b in range(first, end):
-                    multiply(acc[b // PAIR], b)
+                    multiply(acc[i][:, b - first, :], b)
 
-            def keep_base(first):
-                nc.scalar.copy(
-                    out=base[:, first : first + PAIR, :], in_=acc[first // PAIR][:, :PAIR, :]
+            def keep_base(i):
+                first, end = GROUPS[i]
+                nc.scalar.copy(out=base[:, first:end, :], in_=acc[i][:, : end - first, :])
+
+            def hold():
+                nc.tensor.matmul(
+                    acc[-1][:].rearrange("p b o -> p (b o)"),
+                    lhsT=zeros[:, :P],
+                    rhs=zeros[:],
+                    start=True,
+                    stop=True,
                 )
 
             spin(WARM_PASSES)
             w_grouped = flip_w()
             grouped = {}
             grouped[0] = flip_row(0)
-            spin(HOLD_PASSES)
             quantise(w_grouped, w_codes[:], w_scales[:])
             grouped[1] = flip_row(1)
             quantise_row(0, grouped[0])
+            hold()
             grouped[2] = flip_row(2)
             quantise_row(1, grouped[1])
             grouped[3] = flip_row(3)
             quantise_row(2, grouped[2])
             grouped[4] = flip_row(4)
             quantise_row(3, grouped[3])
-            multiply_rows(0, 2)
-            spin(HOLD_PASSES)
-            keep_base(0)
             grouped[5] = flip_row(5)
             quantise_row(4, grouped[4])
+            multiply_group(0)
+            keep_base(0)
             grouped[6] = flip_row(6)
             quantise_row(5, grouped[5])
             grouped[7] = flip_row(7)
             flip_adapters(nc.vector.tensor_copy, 0)
             flip_adapters(nc.vector.tensor_copy, 2)
-            multiply_rows(2, 4)
-            keep_base(2)
             flip_adapters(nc.scalar.copy, 4)
             quantise_row(6, grouped[6])
             flip_adapters(nc.scalar.copy, 6)
             quantise_row(7, grouped[7])
+            multiply_group(1)
+            keep_base(1)
             bank = adapt(0)
             finish(bank, 0, 2)
             finish(bank, 2, 2)
-            multiply_rows(4, 6)
-            keep_base(4)
-            multiply_rows(6, 8)
-            keep_base(6)
+            multiply_group(2)
+            keep_base(2)
             bank = adapt(4)
             finish(bank, 4, 2)
             finish(bank, 6, 2)

@@ -113,8 +113,8 @@ def tile_linear_pa_s_kernel(tc, data, W, t_lora, lora_b, out):
             copy(out=tbT[:, first : first + 2, :, :], in_=bank[:])
 
         def adapt(first):
-            bank = psum.tile([P, BANK, OUT], F32, tag="work", bufs=WORK_BANKS)
-            for i in range(BANK):
+            bank = psum.tile([P, 2, OUT], F32, tag="work", bufs=WORK_BANKS)
+            for i in range(2):
                 nc.tensor.matmul(
                     bank[:, i, :],
                     lhsT=tbT[:, first + i, 0, :],
@@ -124,11 +124,11 @@ def tile_linear_pa_s_kernel(tc, data, W, t_lora, lora_b, out):
                 )
             return bank
 
-        def finish(bank, first, count):
-            these = slice(first, first + count)
+        def finish(bank, first):
+            these = slice(first, first + 2)
             nc.vector.scalar_tensor_tensor(
                 out=result[:, these, :],
-                in0=bank[:, first % BANK : first % BANK + count, :],
+                in0=bank[:],
                 scalar=SCALING,
                 in1=base[:, these, :],
                 op0=mybir.AluOpType.mult,
@@ -195,6 +195,7 @@ def tile_linear_pa_s_kernel(tc, data, W, t_lora, lora_b, out):
             spin(WARM_PASSES)
             w_grouped = flip_w()
             grouped = {}
+            products = {}
             grouped[0] = flip_row(0)
             quantise(w_grouped, w_codes[:], w_scales[:])
             grouped[1] = flip_row(1)
@@ -214,18 +215,20 @@ def tile_linear_pa_s_kernel(tc, data, W, t_lora, lora_b, out):
             quantise_row(5, grouped[5])
             grouped[7] = flip_row(7)
             flip_adapters(nc.vector.tensor_copy, 0)
-            flip_adapters(nc.vector.tensor_copy, 2)
+            flip_adapters(nc.scalar.copy, 2)
             flip_adapters(nc.scalar.copy, 4)
-            quantise_row(6, grouped[6])
             flip_adapters(nc.scalar.copy, 6)
+            products[0] = adapt(0)
+            quantise_row(6, grouped[6])
             quantise_row(7, grouped[7])
+            finish(products[0], 0)
             multiply_group(1)
             keep_base(1)
-            bank = adapt(0)
-            finish(bank, 0, 2)
-            finish(bank, 2, 2)
+            products[2] = adapt(2)
+            finish(products[2], 2)
             multiply_group(2)
             keep_base(2)
-            bank = adapt(4)
-            finish(bank, 4, 2)
-            finish(bank, 6, 2)
+            products[4] = adapt(4)
+            finish(products[4], 4)
+            products[6] = adapt(6)
+            finish(products[6], 6)

from contextlib import ExitStack

import concourse.mybir as mybir
from concourse.masks import make_identity

BF16 = mybir.dt.bfloat16
F32 = mybir.dt.float32
U32 = mybir.dt.uint32
U8 = mybir.dt.uint8
FP8X4 = mybir.dt.float8_e4m3fn_x4

P = 128
B, S, IN, OUT, R = 8, 128, 1024, 128, 128
SCALING = 2.0

PACK = 4
PASSES = IN // (P * PACK)
PAIR = 2
WORDS = IN // PAIR
HALVES = PACK // PAIR
BANK = 4
GROUPS = [(0, 4), (4, 6), (6, 8)]
WARM_PASSES = 12
WORK_BANKS = 5

FLOPS = 2 * B * S * IN * OUT + 2 * B * S * R * OUT


def tile_linear_pa_s_kernel(tc, data, W, t_lora, lora_b, out):
    nc = tc.nc
    with ExitStack() as ctx:
        keep = ctx.enter_context(tc.tile_pool(name="keep", bufs=1))
        stage = ctx.enter_context(tc.tile_pool(name="stage", bufs=6))
        psum = ctx.enter_context(tc.psum_pool(name="psum", bufs=1))

        ident_f32 = keep.tile([P, P], F32)
        make_identity(nc, ident_f32[:])
        ident_bf16 = keep.tile([P, P], BF16)
        make_identity(nc, ident_bf16[:])

        w_sb = [keep.tile([P, IN // PASSES], BF16, name=f"w_sb{g}") for g in range(PASSES)]
        x_sb = keep.tile([P, B, IN], BF16)
        t_sb = keep.tile([P, B, R], BF16)
        b_sb = keep.tile([P, B, R], BF16)

        def load_adapters(first, count):
            these = slice(first, first + count)
            nc.sync.dma_start(
                out=t_sb[:, these, :], in_=t_lora[these].rearrange("a g s r -> s (a g) r")
            )
            nc.sync.dma_start(out=b_sb[:, these, :], in_=lora_b[these].rearrange("a o r -> o a r"))

        for g in range(PASSES):
            nc.sync.dma_start(out=w_sb[g][:], in_=W[:, g * P * PACK : (g + 1) * P * PACK])
        for b in range(B):
            nc.sync.dma_start(out=x_sb[:, b, :], in_=data[b, :, :])
        for first in range(0, B, BANK):
            load_adapters(first, BANK)

        w_codes = keep.tile([P, PASSES * OUT], U32, align_bytes=64)
        w_scales = keep.tile([P, PASSES * OUT], U8, align_bytes=64)
        x_codes = keep.tile([P, B, PASSES * S], U32, align_bytes=64)
        x_scales = keep.tile([P, B, PASSES * S], U8, align_bytes=64)
        tbT = keep.tile([P, B, 2, P], BF16)
        base = keep.tile([P, B, OUT], F32)
        result = keep.tile([P, B, OUT], F32)

        def flip_pass(half_bank, words):
            for u in range(HALVES):
                nc.tensor.transpose(half_bank[:, u, :], words[:, u::HALVES], ident_f32[:])

        def flip(words):
            bank = psum.tile([P, PASSES * HALVES, P], F32, tag="work", bufs=WORK_BANKS)
            for g in range(PASSES):
                words_of_pass = words[:, g * HALVES * P : (g + 1) * HALVES * P]
                flip_pass(bank[:, g * HALVES : (g + 1) * HALVES, :], words_of_pass)
            return bank

        def regroup(copy, bank):
            grouped = stage.tile([P, PASSES * P * PACK], BF16, align_bytes=64, tag="grouped")
            copy(
                out=grouped[:].bitcast(F32).rearrange("p (g r u) -> p g r u", g=PASSES, u=HALVES),
                in_=bank[:].rearrange("p (g u) r -> p g r u", u=HALVES),
            )
            return grouped[:]

        def quantise(grouped, codes, scales):
            nc.vector.quantize_mx(out=codes.bitcast(FP8X4), scales=scales, in_=grouped)

        def flip_row(b):
            return regroup(nc.scalar.copy, flip(x_sb[:, b, :].bitcast(F32)))

        def quantise_row(b, grouped):
            quantise(grouped, x_codes[:, b, :], x_scales[:, b, :])

        def multiply(product, b):
            for g in range(PASSES):
                nc.tensor.matmul_mx(
                    out=product,
                    lhsT=x_codes[:, b, g * S : (g + 1) * S].bitcast(FP8X4),
                    lhsT_scale=x_scales[:, b, g * S : (g + 1) * S],
                    rhs=w_codes[:, g * OUT : (g + 1) * OUT].bitcast(FP8X4),
                    rhs_scale=w_scales[:, g * OUT : (g + 1) * OUT],
                    start=(g == 0),
                    stop=(g == PASSES - 1),
                )

        def flip_adapters(copy, first):
            bank = psum.tile([P, 2, 2, P], BF16, tag="work", bufs=WORK_BANKS)
            for i in range(2):
                nc.tensor.transpose(bank[:, i, 0, :], t_sb[:, first + i, :], ident_bf16[:])
                nc.tensor.transpose(bank[:, i, 1, :], b_sb[:, first + i, :], ident_bf16[:])
            copy(out=tbT[:, first : first + 2, :, :], in_=bank[:])

        def adapt(first):
            bank = psum.tile([P, 2, OUT], F32, tag="work", bufs=WORK_BANKS)
            for i in range(2):
                nc.tensor.matmul(
                    bank[:, i, :],
                    lhsT=tbT[:, first + i, 0, :],
                    rhs=tbT[:, first + i, 1, :],
                    start=True,
                    stop=True,
                )
            return bank

        def finish(bank, first):
            these = slice(first, first + 2)
            nc.vector.scalar_tensor_tensor(
                out=result[:, these, :],
                in0=bank[:],
                scalar=SCALING,
                in1=base[:, these, :],
                op0=mybir.AluOpType.mult,
                op1=mybir.AluOpType.add,
            )
            nc.sync.dma_start(out=out[these].rearrange("b s o -> s b o"), in_=result[:, these, :])

        with tc.manual_schedule():
            zeros = keep.tile([P, P * PACK], BF16, align_bytes=64)
            nc.vector.memset(zeros[:].bitcast(U32), 0)
            zero_codes = keep.tile([P, P], U32, align_bytes=64)
            zero_scales = keep.tile([P, P], U8, align_bytes=64)
            nc.vector.quantize_mx(
                out=zero_codes[:].bitcast(FP8X4), scales=zero_scales[:], in_=zeros[:]
            )

            acc = [
                psum.tile([P, BANK, OUT], F32, tag="mx", bufs=len(GROUPS), name="acc")
                for group in GROUPS
            ]

            def spin(count):
                for i in range(count):
                    nc.tensor.matmul_mx(
                        out=acc[-1][:, 0, :],
                        lhsT=zero_codes[:].bitcast(FP8X4),
                        lhsT_scale=zero_scales[:],
                        rhs=zero_codes[:].bitcast(FP8X4),
                        rhs_scale=zero_scales[:],
                        start=True,
                        stop=True,
                    )


            def flip_w():
                grouped = stage.tile([P, PASSES, P * PACK], BF16, align_bytes=64, tag="grouped")
                for g in range(PASSES):
                    bank = psum.tile([P, HALVES, P], F32, tag="work", bufs=WORK_BANKS)
                    flip_pass(bank, w_sb[g][:].bitcast(F32))
                    nc.scalar.copy(
                        out=grouped[:, g, :].bitcast(F32).rearrange("p (r u) -> p r u", u=HALVES),
                        in_=bank[:].rearrange("p u r -> p r u"),
                    )
                return grouped[:].rearrange("p g c -> p (g c)")

            def multiply_group(i):
                first, end = GROUPS[i]
                for b in range(first, end):
                    multiply(acc[i][:, b - first, :], b)

            def keep_base(i):
                first, end = GROUPS[i]
                nc.scalar.copy(out=base[:, first:end, :], in_=acc[i][:, : end - first, :])

            def hold():
                nc.tensor.matmul(
                    acc[-1][:].rearrange("p b o -> p (b o)"),
                    lhsT=zeros[:, :P],
                    rhs=zeros[:],
                    start=True,
                    stop=True,
                )

            spin(WARM_PASSES)
            w_grouped = flip_w()
            grouped = {}
            products = {}
            grouped[0] = flip_row(0)
            quantise(w_grouped, w_codes[:], w_scales[:])
            grouped[1] = flip_row(1)
            quantise_row(0, grouped[0])
            hold()
            grouped[2] = flip_row(2)
            quantise_row(1, grouped[1])
            grouped[3] = flip_row(3)
            quantise_row(2, grouped[2])
            grouped[4] = flip_row(4)
            quantise_row(3, grouped[3])
            grouped[5] = flip_row(5)
            quantise_row(4, grouped[4])
            multiply_group(0)
            keep_base(0)
            grouped[6] = flip_row(6)
            quantise_row(5, grouped[5])
            grouped[7] = flip_row(7)
            flip_adapters(nc.vector.tensor_copy, 0)
            flip_adapters(nc.scalar.copy, 2)
            flip_adapters(nc.scalar.copy, 4)
            flip_adapters(nc.scalar.copy, 6)
            products[0] = adapt(0)
            quantise_row(6, grouped[6])
            quantise_row(7, grouped[7])
            finish(products[0], 0)
            multiply_group(1)
            keep_base(1)
            products[2] = adapt(2)
            finish(products[2], 2)
            multiply_group(2)
            keep_base(2)
            products[4] = adapt(4)
            finish(products[4], 4)
            products[6] = adapt(6)
            finish(products[6], 6)
